import numpy as np
import ml_dtypes


def mxq(x, axis, fmt="e4m3"):
    dtype, down = {"e4m3": (ml_dtypes.float8_e4m3fn, 7), "e5m2": (ml_dtypes.float8_e5m2, 14)}[fmt]
    v = np.moveaxis(np.asarray(x, np.float32).astype(ml_dtypes.bfloat16).astype(np.float64), axis, -1)
    blocks = v.reshape(v.shape[:-1] + (-1, 32))
    amax = np.abs(blocks).max(-1, keepdims=True)
    byte = np.maximum(np.where(amax > 0, np.frexp(amax)[1] - 1 + 127, 0) - down, 1)
    scale = np.exp2(byte - 127.0)
    codes = (blocks / scale).astype(np.float32).astype(dtype).astype(np.float64)
    return np.moveaxis((codes * scale).reshape(v.shape), -1, axis)


WIDE = False


def mx_kscale(k):
    if not WIDE:
        return np.ones(k)
    levels = np.array([10, -10, 5, -5, 0])
    a = np.random.permutation(np.resize(levels, k // 512 * 4)).reshape(k // 512, 4)
    idx = np.arange(k)
    return np.exp2(a[idx // 512, idx % 128 // 32])


BF16 = ml_dtypes.bfloat16


def bf(x):
    return np.asarray(x, np.float32).astype(BF16)


def f64(x):
    return np.asarray(x).astype(np.float64)


B, S, H, HD = 4, 256, 8, 128
D = H * HD
HALF = HD // 2


def apply_rope(t, cos, sin):
    t0 = t[..., 0::2]
    t1 = t[..., 1::2]
    out0 = t0 * cos - t1 * sin
    out1 = t0 * sin + t1 * cos
    return np.stack([out0, out1], axis=-1).reshape(t.shape)


def setup_inputs():
    s = mx_kscale(D)
    phi = np.random.uniform(0.0, 2.0 * np.pi, (S, HALF))
    return {"x": bf(np.random.standard_normal((B, S, D)) * s),
            "w_qkv": bf(np.random.standard_normal((D, 3 * D)) / np.sqrt(D) / s[:, None]),
            "cos": bf(np.cos(phi)), "sin": bf(np.sin(phi))}


def reference(x, w_qkv, cos, sin):
    qkv = mxq(f64(x), 2, "e4m3") @ mxq(f64(w_qkv), 0, "e4m3")
    qkv = qkv.reshape(B, S, 3, H, HD).transpose(2, 0, 3, 1, 4)
    q, k, v = qkv[0], qkv[1], qkv[2]
    c, sn = f64(cos), f64(sin)
    return apply_rope(q, c, sn), apply_rope(k, c, sn), np.ascontiguousarray(v)

@@ -1,0 +1,178 @@
+from contextlib import ExitStack
+
+import concourse.mybir as mybir
+from concourse.masks import make_identity
+
+F32 = mybir.dt.float32
+BF16 = mybir.dt.bfloat16
+U32 = mybir.dt.uint32
+U8 = mybir.dt.uint8
+FP8X4 = mybir.dt.float8_e4m3fn_x4
+MULT = mybir.AluOpType.mult
+ADD = mybir.AluOpType.add
+
+B, S, H, HD = 4, 256, 8, 128
+D = H * HD
+PAIRS = HD // 2
+P = 128
+PACK = 4
+K_PASS = P * PACK
+PASSES = D // K_PASS
+POS = S // P
+TOKEN_TILES = B * POS
+CHUNK = 512
+CHUNK_HEADS = CHUNK // HD
+HALVES = D // CHUNK
+Q = 0
+K = 1
+V = 2
+
+FLOPS = 2 * B * S * D * 3 * D
+
+
+def tile_ropeflashattention_pa_kernel(tc, x, w_qkv, cos, sin, out_0, out_1, out_2):
+    nc = tc.nc
+    outs = (out_0, out_1, out_2)
+    chunks = [(which, half) for half in range(HALVES) for which in (Q, V, K)]
+
+    with ExitStack() as ctx:
+        keep = ctx.enter_context(tc.tile_pool(name="keep", bufs=1))
+        w_rows = ctx.enter_context(tc.tile_pool(name="w_rows", bufs=len(chunks)))
+        w_grouped = ctx.enter_context(tc.tile_pool(name="w_grouped", bufs=4))
+        products = ctx.enter_context(tc.tile_pool(name="products", bufs=4))
+        results = ctx.enter_context(tc.tile_pool(name="results", bufs=6))
+        banks = ctx.enter_context(tc.psum_pool(name="banks", bufs=6))
+        v_banks = ctx.enter_context(tc.psum_pool(name="v_banks", bufs=2))
+
+        cos_sb = keep.tile([P, POS, PAIRS], BF16)
+        sin_sb = keep.tile([P, POS, PAIRS], BF16)
+        nc.scalar.dma_start(out=cos_sb[:], in_=cos.rearrange("(p t) j -> p t j", t=POS))
+        nc.scalar.dma_start(out=sin_sb[:], in_=sin.rearrange("(p t) j -> p t j", t=POS))
+
+        x_sb = keep.tile([P, B, POS, D], BF16)
+
+        def load_x(b):
+            nc.sync.dma_start(out=x_sb[:, b], in_=x[b].rearrange("(p t) k -> p t k", t=POS))
+
+        def load_w(which, half):
+            col = which * D + half * CHUNK
+            rows = w_rows.tile([P, PASSES, PACK, CHUNK], BF16, name="rows")
+            for g in range(PASSES):
+                nc.sync.dma_start(
+                    out=rows[:, g],
+                    in_=w_qkv[g * K_PASS : (g + 1) * K_PASS, col : col + CHUNK].rearrange(
+                        "(p f) n -> p f n", f=PACK
+                    ),
+                )
+            return rows
+
+        load_x(0)
+        w_chunk_rows = [load_w(*chunks[0])]
+        for b in range(1, B):
+            load_x(b)
+        for which, half in chunks[1:]:
+            w_chunk_rows.append(load_w(which, half))
+
+        identity = keep.tile([P, P], F32)
+        make_identity(nc, identity[:])
+
+        rotation = keep.tile([P, POS, 2, PAIRS, 2], F32)
+        nc.gpsimd.tensor_copy(out=rotation[:, :, 0, :, 0], in_=cos_sb[:])
+        nc.gpsimd.tensor_copy(out=rotation[:, :, 0, :, 1], in_=sin_sb[:])
+        nc.gpsimd.tensor_scalar_mul(out=rotation[:, :, 1, :, 0], in0=sin_sb[:], scalar1=-1.0)
+        nc.gpsimd.tensor_copy(out=rotation[:, :, 1, :, 1], in_=cos_sb[:])
+
+        x_grouped = keep.tile([P, TOKEN_TILES, PASSES, P, PACK], BF16, align_bytes=64)
+        x_codes = keep.tile([P, TOKEN_TILES, PASSES, P], U32, align_bytes=64)
+        x_scales = keep.tile([P, TOKEN_TILES, PASSES, P], U8, align_bytes=64)
+        for b in range(B):
+            for t in range(POS):
+                i = b * POS + t
+                words = x_sb[:, b, t, :].bitcast(F32).rearrange(
+                    "m (g p u) -> m g u p", g=PASSES, u=2
+                )
+                flipped = banks.tile([P, PASSES, 2, P], F32, tag="bank")
+                for g in range(PASSES):
+                    for u in range(2):
+                        nc.tensor.transpose(flipped[:, g, u, :], words[:, g, u, :], identity[:])
+                nc.scalar.copy(
+                    out=x_grouped[:, i]
+                    .rearrange("p g m f -> p (g m f)")
+                    .bitcast(F32)
+                    .rearrange("p (g m u) -> p g m u", g=PASSES, u=2),
+                    in_=flipped[:].rearrange("p g u m -> p g m u"),
+                )
+            both = slice(b * POS, (b + 1) * POS)
+            nc.vector.quantize_mx(
+                out=x_codes[:, both].rearrange("p i g m -> p (i g m)").bitcast(FP8X4),
+                scales=x_scales[:, both].rearrange("p i g m -> p (i g m)"),
+                in_=x_grouped[:, both].rearrange("p i g m f -> p (i g m f)"),
+            )
+
+        w_codes = keep.tile([P, len(chunks), PASSES, CHUNK], U32, align_bytes=64)
+        w_scales = keep.tile([P, len(chunks), PASSES, CHUNK], U8, align_bytes=64)
+
+        for c, (which, half) in enumerate(chunks):
+            copy = nc.vector.tensor_copy if c == 0 else nc.scalar.copy
+            for g in range(PASSES):
+                grouped = w_grouped.tile([P, CHUNK, PACK], BF16, align_bytes=64)
+                copy(
+                    out=grouped[:].rearrange("p (n i) f -> p n f i", i=4),
+                    in_=w_chunk_rows[c][:, g].rearrange("p f (n i) -> p n f i", i=4),
+                )
+                nc.vector.quantize_mx(
+                    out=w_codes[:, c, g, :].bitcast(FP8X4),
+                    scales=w_scales[:, c, g, :],
+                    in_=grouped[:].rearrange("p n f -> p (n f)"),
+                )
+
+            for b in range(B):
+                result = results.tile([P, CHUNK_HEADS, POS, HD], F32)
+                for t in range(POS):
+                    i = b * POS + t
+                    if which == V:
+                        sums = v_banks.tile([P, CHUNK], F32, tag="v_bank")
+                    else:
+                        sums = banks.tile([P, CHUNK], F32, tag="bank")
+                    for g in range(PASSES):
+                        nc.tensor.matmul_mx(
+                            out=sums[:],
+                            lhsT=x_codes[:, i, g, :].bitcast(FP8X4),
+                            lhsT_scale=x_scales[:, i, g, :],
+                            rhs=w_codes[:, c, g, :].bitcast(FP8X4),
+                            rhs_scale=w_scales[:, c, g, :],
+                            start=(g == 0),
+                            stop=(g == PASSES - 1),
+                        )
+                    if which == V:
+                        nc.scalar.copy(
+                            out=result[:, :, t, :],
+                            in_=sums[:].rearrange("p (h d) -> p h d", h=CHUNK_HEADS),
+                        )
+                        continue
+                    shape = [P, 2, CHUNK_HEADS, PAIRS, 2]
+                    product = products.tile([P, 2, CHUNK], F32)
+                    nc.vector.tensor_tensor(
+                        out=product[:].rearrange(
+                            "p e (h j r) -> p e h j r", h=CHUNK_HEADS, r=2
+                        ),
+                        in0=sums[:]
+                        .rearrange("p (h j e) -> p e h j", h=CHUNK_HEADS, e=2)
+                        .unsqueeze(4)
+                        .to_broadcast(shape),
+                        in1=rotation[:, t].unsqueeze(2).to_broadcast(shape),
+                        op=MULT,
+                    )
+                    nc.gpsimd.tensor_tensor(
+                        out=result[:, :, t, :],
+                        in0=product[:, 0, :].rearrange("p (h d) -> p h d", h=CHUNK_HEADS),
+                        in1=product[:, 1, :].rearrange("p (h d) -> p h d", h=CHUNK_HEADS),
+                        op=ADD,
+                    )
+                first_head = half * CHUNK_HEADS
+                nc.sync.dma_start(
+                    out=outs[which][b, first_head : first_head + CHUNK_HEADS].rearrange(
+                        "h (p t) d -> p h (t d)", t=POS
+                    ),
+                    in_=result[:].rearrange("p h t d -> p h (t d)"),
+                )

@@ -33,13 +33,13 @@ FLOPS = 2 * B * S * D * 3 * D
 def tile_ropeflashattention_pa_kernel(tc, x, w_qkv, cos, sin, out_0, out_1, out_2):
     nc = tc.nc
     outs = (out_0, out_1, out_2)
-    chunks = [(which, half) for half in range(HALVES) for which in (Q, V, K)]
+    chunks = [(Q, 0), (K, 0), (V, 0), (Q, 1), (V, 1), (K, 1)]
 
     with ExitStack() as ctx:
         keep = ctx.enter_context(tc.tile_pool(name="keep", bufs=1))
         w_rows = ctx.enter_context(tc.tile_pool(name="w_rows", bufs=len(chunks)))
         w_grouped = ctx.enter_context(tc.tile_pool(name="w_grouped", bufs=4))
-        products = ctx.enter_context(tc.tile_pool(name="products", bufs=4))
+        products = ctx.enter_context(tc.tile_pool(name="products", bufs=3))
         results = ctx.enter_context(tc.tile_pool(name="results", bufs=6))
         banks = ctx.enter_context(tc.psum_pool(name="banks", bufs=6))
         v_banks = ctx.enter_context(tc.psum_pool(name="v_banks", bufs=2))
@@ -66,9 +66,8 @@ def tile_ropeflashattention_pa_kernel(tc, x, w_qkv, cos, sin, out_0, out_1, out_
                 )
             return rows
 
-        load_x(0)
         w_chunk_rows = [load_w(*chunks[0])]
-        for b in range(1, B):
+        for b in range(B):
             load_x(b)
         for which, half in chunks[1:]:
             w_chunk_rows.append(load_w(which, half))
@@ -85,7 +84,10 @@ def tile_ropeflashattention_pa_kernel(tc, x, w_qkv, cos, sin, out_0, out_1, out_
         x_grouped = keep.tile([P, TOKEN_TILES, PASSES, P, PACK], BF16, align_bytes=64)
         x_codes = keep.tile([P, TOKEN_TILES, PASSES, P], U32, align_bytes=64)
         x_scales = keep.tile([P, TOKEN_TILES, PASSES, P], U8, align_bytes=64)
-        for b in range(B):
+        w_codes = keep.tile([P, len(chunks), PASSES, CHUNK], U32, align_bytes=64)
+        w_scales = keep.tile([P, len(chunks), PASSES, CHUNK], U8, align_bytes=64)
+
+        def quantise_x(b):
             for t in range(POS):
                 i = b * POS + t
                 words = x_sb[:, b, t, :].bitcast(F32).rearrange(
@@ -102,58 +104,59 @@ def tile_ropeflashattention_pa_kernel(tc, x, w_qkv, cos, sin, out_0, out_1, out_
                     .rearrange("p (g m u) -> p g m u", g=PASSES, u=2),
                     in_=flipped[:].rearrange("p g u m -> p g m u"),
                 )
-            both = slice(b * POS, (b + 1) * POS)
-            nc.vector.quantize_mx(
-                out=x_codes[:, both].rearrange("p i g m -> p (i g m)").bitcast(FP8X4),
-                scales=x_scales[:, both].rearrange("p i g m -> p (i g m)"),
-                in_=x_grouped[:, both].rearrange("p i g m f -> p (i g m f)"),
-            )
+                nc.vector.quantize_mx(
+                    out=x_codes[:, i].rearrange("p g m -> p (g m)").bitcast(FP8X4),
+                    scales=x_scales[:, i].rearrange("p g m -> p (g m)"),
+                    in_=x_grouped[:, i].rearrange("p g m f -> p (g m f)"),
+                )
 
-        w_codes = keep.tile([P, len(chunks), PASSES, CHUNK], U32, align_bytes=64)
-        w_scales = keep.tile([P, len(chunks), PASSES, CHUNK], U8, align_bytes=64)
-
-        for c, (which, half) in enumerate(chunks):
+        def quantise_w(c):
             copy = nc.vector.tensor_copy if c == 0 else nc.scalar.copy
+            grouped = []
             for g in range(PASSES):
-                grouped = w_grouped.tile([P, CHUNK, PACK], BF16, align_bytes=64)
+                grouped.append(w_grouped.tile([P, CHUNK, PACK], BF16, align_bytes=64, name="grouped"))
                 copy(
-                    out=grouped[:].rearrange("p (n i) f -> p n f i", i=4),
+                    out=grouped[g][:].rearrange("p (n i) f -> p n f i", i=4),
                     in_=w_chunk_rows[c][:, g].rearrange("p f (n i) -> p n f i", i=4),
                 )
+            for g in range(PASSES):
                 nc.vector.quantize_mx(
                     out=w_codes[:, c, g, :].bitcast(FP8X4),
                     scales=w_scales[:, c, g, :],
-                    in_=grouped[:].rearrange("p n f -> p (n f)"),
+                    in_=grouped[g][:].rearrange("p n f -> p (n f)"),
                 )
 
-            for b in range(B):
-                result = results.tile([P, CHUNK_HEADS, POS, HD], F32)
-                for t in range(POS):
-                    i = b * POS + t
-                    if which == V:
-                        sums = v_banks.tile([P, CHUNK], F32, tag="v_bank")
-                    else:
-                        sums = banks.tile([P, CHUNK], F32, tag="bank")
-                    for g in range(PASSES):
-                        nc.tensor.matmul_mx(
-                            out=sums[:],
-                            lhsT=x_codes[:, i, g, :].bitcast(FP8X4),
-                            lhsT_scale=x_scales[:, i, g, :],
-                            rhs=w_codes[:, c, g, :].bitcast(FP8X4),
-                            rhs_scale=w_scales[:, c, g, :],
-                            start=(g == 0),
-                            stop=(g == PASSES - 1),
-                        )
-                    if which == V:
-                        nc.scalar.copy(
-                            out=result[:, :, t, :],
-                            in_=sums[:].rearrange("p (h d) -> p h d", h=CHUNK_HEADS),
-                        )
-                        continue
+        def multiply(c, b):
+            which, half = chunks[c]
+            result = results.tile([P, CHUNK_HEADS, POS, HD], F32)
+            product = None
+            if which != V:
+                product = products.tile([P, POS, 2, CHUNK], F32)
+            for t in range(POS):
+                i = b * POS + t
+                if which == V:
+                    sums = v_banks.tile([P, CHUNK], F32, tag="v_bank")
+                else:
+                    sums = banks.tile([P, CHUNK], F32, tag="bank")
+                for g in range(PASSES):
+                    nc.tensor.matmul_mx(
+                        out=sums[:],
+                        lhsT=x_codes[:, i, g, :].bitcast(FP8X4),
+                        lhsT_scale=x_scales[:, i, g, :],
+                        rhs=w_codes[:, c, g, :].bitcast(FP8X4),
+                        rhs_scale=w_scales[:, c, g, :],
+                        start=(g == 0),
+                        stop=(g == PASSES - 1),
+                    )
+                if which == V:
+                    nc.scalar.copy(
+                        out=result[:, :, t, :],
+                        in_=sums[:].rearrange("p (h d) -> p h d", h=CHUNK_HEADS),
+                    )
+                else:
                     shape = [P, 2, CHUNK_HEADS, PAIRS, 2]
-                    product = products.tile([P, 2, CHUNK], F32)
                     nc.vector.tensor_tensor(
-                        out=product[:].rearrange(
+                        out=product[:, t].rearrange(
                             "p e (h j r) -> p e h j r", h=CHUNK_HEADS, r=2
                         ),
                         in0=sums[:]
@@ -163,16 +166,35 @@ def tile_ropeflashattention_pa_kernel(tc, x, w_qkv, cos, sin, out_0, out_1, out_
                         in1=rotation[:, t].unsqueeze(2).to_broadcast(shape),
                         op=MULT,
                     )
-                    nc.gpsimd.tensor_tensor(
-                        out=result[:, :, t, :],
-                        in0=product[:, 0, :].rearrange("p (h d) -> p h d", h=CHUNK_HEADS),
-                        in1=product[:, 1, :].rearrange("p (h d) -> p h d", h=CHUNK_HEADS),
-                        op=ADD,
-                    )
-                first_head = half * CHUNK_HEADS
-                nc.sync.dma_start(
-                    out=outs[which][b, first_head : first_head + CHUNK_HEADS].rearrange(
-                        "h (p t) d -> p h (t d)", t=POS
-                    ),
-                    in_=result[:].rearrange("p h t d -> p h (t d)"),
+            if which != V:
+                last = c == len(chunks) - 1 and b == B - 1
+                adder = nc.vector if last else nc.gpsimd
+                adder.tensor_tensor(
+                    out=result[:].rearrange("p h t d -> p t h d"),
+                    in0=product[:, :, 0, :].rearrange("p t (h d) -> p t h d", h=CHUNK_HEADS),
+                    in1=product[:, :, 1, :].rearrange("p t (h d) -> p t h d", h=CHUNK_HEADS),
+                    op=ADD,
                 )
+            first_head = half * CHUNK_HEADS
+            nc.sync.dma_start(
+                out=outs[which][b, first_head : first_head + CHUNK_HEADS].rearrange(
+                    "h (p t) d -> p h (t d)", t=POS
+                ),
+                in_=result[:].rearrange("p h t d -> p h (t d)"),
+            )
+
+        AHEAD = 2
+        quantise_w(0)
+        for b in range(AHEAD):
+            quantise_x(b)
+        for b in range(B):
+            if b + AHEAD < B:
+                quantise_x(b + AHEAD)
+            else:
+                quantise_w(b + AHEAD - B + 1)
+            multiply(0, b)
+        for c in range(1, len(chunks)):
+            if c + AHEAD < len(chunks):
+                quantise_w(c + AHEAD)
+            for b in range(B):
+                multiply(c, b)

@@ -167,7 +167,7 @@ def tile_ropeflashattention_pa_kernel(tc, x, w_qkv, cos, sin, out_0, out_1, out_
                         op=MULT,
                     )
             if which != V:
-                last = c == len(chunks) - 1 and b == B - 1
+                last = c in (1, 3, 5) and b == B - 1
                 adder = nc.vector if last else nc.gpsimd
                 adder.tensor_tensor(
                     out=result[:].rearrange("p h t d -> p t h d"),

@@ -38,7 +38,7 @@ def tile_ropeflashattention_pa_kernel(tc, x, w_qkv, cos, sin, out_0, out_1, out_
     with ExitStack() as ctx:
         keep = ctx.enter_context(tc.tile_pool(name="keep", bufs=1))
         w_rows = ctx.enter_context(tc.tile_pool(name="w_rows", bufs=len(chunks)))
-        w_grouped = ctx.enter_context(tc.tile_pool(name="w_grouped", bufs=4))
+        w_grouped = ctx.enter_context(tc.tile_pool(name="w_grouped", bufs=2))
         products = ctx.enter_context(tc.tile_pool(name="products", bufs=3))
         results = ctx.enter_context(tc.tile_pool(name="results", bufs=6))
         banks = ctx.enter_context(tc.psum_pool(name="banks", bufs=6))
@@ -75,11 +75,11 @@ def tile_ropeflashattention_pa_kernel(tc, x, w_qkv, cos, sin, out_0, out_1, out_
         identity = keep.tile([P, P], F32)
         make_identity(nc, identity[:])
 
-        rotation = keep.tile([P, POS, 2, PAIRS, 2], F32)
-        nc.gpsimd.tensor_copy(out=rotation[:, :, 0, :, 0], in_=cos_sb[:])
-        nc.gpsimd.tensor_copy(out=rotation[:, :, 0, :, 1], in_=sin_sb[:])
-        nc.gpsimd.tensor_scalar_mul(out=rotation[:, :, 1, :, 0], in0=sin_sb[:], scalar1=-1.0)
-        nc.gpsimd.tensor_copy(out=rotation[:, :, 1, :, 1], in_=cos_sb[:])
+        rotation = keep.tile([P, POS, 2, PAIRS, 2], BF16)
+        nc.scalar.copy(out=rotation[:, :, 0, :, 0], in_=cos_sb[:])
+        nc.scalar.copy(out=rotation[:, :, 0, :, 1], in_=sin_sb[:])
+        nc.scalar.mul(out=rotation[:, :, 1, :, 0], in_=sin_sb[:], mul=-1.0)
+        nc.scalar.copy(out=rotation[:, :, 1, :, 1], in_=cos_sb[:])
 
         x_grouped = keep.tile([P, TOKEN_TILES, PASSES, P, PACK], BF16, align_bytes=64)
         x_codes = keep.tile([P, TOKEN_TILES, PASSES, P], U32, align_bytes=64)
@@ -112,18 +112,24 @@ def tile_ropeflashattention_pa_kernel(tc, x, w_qkv, cos, sin, out_0, out_1, out_
 
         def quantise_w(c):
             copy = nc.vector.tensor_copy if c == 0 else nc.scalar.copy
-            grouped = []
+            grouped = w_grouped.tile([P, PASSES, CHUNK, PACK], BF16, align_bytes=64)
             for g in range(PASSES):
-                grouped.append(w_grouped.tile([P, CHUNK, PACK], BF16, align_bytes=64, name="grouped"))
                 copy(
-                    out=grouped[g][:].rearrange("p (n i) f -> p n f i", i=4),
+                    out=grouped[:, g].rearrange("p (n i) f -> p n f i", i=4),
                     in_=w_chunk_rows[c][:, g].rearrange("p f (n i) -> p n f i", i=4),
                 )
-            for g in range(PASSES):
+            if c < 3:
+                for g in range(PASSES):
+                    nc.vector.quantize_mx(
+                        out=w_codes[:, c, g, :].bitcast(FP8X4),
+                        scales=w_scales[:, c, g, :],
+                        in_=grouped[:, g].rearrange("p n f -> p (n f)"),
+                    )
+            else:
                 nc.vector.quantize_mx(
-                    out=w_codes[:, c, g, :].bitcast(FP8X4),
-                    scales=w_scales[:, c, g, :],
-                    in_=grouped[g][:].rearrange("p n f -> p (n f)"),
+                    out=w_codes[:, c].rearrange("p g n -> p (g n)").bitcast(FP8X4),
+                    scales=w_scales[:, c].rearrange("p g n -> p (g n)"),
+                    in_=grouped[:].rearrange("p g n f -> p (g n f)"),
                 )
 
         def multiply(c, b):

@@ -75,11 +75,11 @@ def tile_ropeflashattention_pa_kernel(tc, x, w_qkv, cos, sin, out_0, out_1, out_
         identity = keep.tile([P, P], F32)
         make_identity(nc, identity[:])
 
-        rotation = keep.tile([P, POS, 2, PAIRS, 2], BF16)
+        rotation = keep.tile([P, POS, 2, PAIRS, 2], F32)
         nc.scalar.copy(out=rotation[:, :, 0, :, 0], in_=cos_sb[:])
         nc.scalar.copy(out=rotation[:, :, 0, :, 1], in_=sin_sb[:])
-        nc.scalar.mul(out=rotation[:, :, 1, :, 0], in_=sin_sb[:], mul=-1.0)
-        nc.scalar.copy(out=rotation[:, :, 1, :, 1], in_=cos_sb[:])
+        nc.vector.tensor_scalar_mul(out=rotation[:, :, 1, :, 0], in0=sin_sb[:], scalar1=-1.0)
+        nc.vector.tensor_copy(out=rotation[:, :, 1, :, 1], in_=cos_sb[:])
 
         x_grouped = keep.tile([P, TOKEN_TILES, PASSES, P, PACK], BF16, align_bytes=64)
         x_codes = keep.tile([P, TOKEN_TILES, PASSES, P], U32, align_bytes=64)

@@ -39,8 +39,9 @@ def tile_ropeflashattention_pa_kernel(tc, x, w_qkv, cos, sin, out_0, out_1, out_
         keep = ctx.enter_context(tc.tile_pool(name="keep", bufs=1))
         w_rows = ctx.enter_context(tc.tile_pool(name="w_rows", bufs=len(chunks)))
         w_grouped = ctx.enter_context(tc.tile_pool(name="w_grouped", bufs=2))
-        products = ctx.enter_context(tc.tile_pool(name="products", bufs=3))
+        products = ctx.enter_context(tc.tile_pool(name="products", bufs=4))
         results = ctx.enter_context(tc.tile_pool(name="results", bufs=6))
+        v_results = ctx.enter_context(tc.tile_pool(name="v_results", bufs=B))
         banks = ctx.enter_context(tc.psum_pool(name="banks", bufs=6))
         v_banks = ctx.enter_context(tc.psum_pool(name="v_banks", bufs=2))
 
@@ -132,12 +133,20 @@ def tile_ropeflashattention_pa_kernel(tc, x, w_qkv, cos, sin, out_0, out_1, out_
                     in_=grouped[:].rearrange("p g n f -> p (g n f)"),
                 )
 
+        TENSOR_ADDS = ((3, B - 1),)
+        held = {}
+
         def multiply(c, b):
             which, half = chunks[c]
-            result = results.tile([P, CHUNK_HEADS, POS, HD], F32)
             product = None
             if which != V:
                 product = products.tile([P, POS, 2, CHUNK], F32)
+            if (c, b) in TENSOR_ADDS:
+                result = None
+                held[(c, b)] = product
+            else:
+                result_pool = v_results if which == V else results
+                result = result_pool.tile([P, CHUNK_HEADS, POS, HD], F32)
             for t in range(POS):
                 i = b * POS + t
                 if which == V:
@@ -172,22 +181,53 @@ def tile_ropeflashattention_pa_kernel(tc, x, w_qkv, cos, sin, out_0, out_1, out_
                         in1=rotation[:, t].unsqueeze(2).to_broadcast(shape),
                         op=MULT,
                     )
-            if which != V:
-                last = c in (1, 3, 5) and b == B - 1
-                adder = nc.vector if last else nc.gpsimd
-                adder.tensor_tensor(
-                    out=result[:].rearrange("p h t d -> p t h d"),
-                    in0=product[:, :, 0, :].rearrange("p t (h d) -> p t h d", h=CHUNK_HEADS),
-                    in1=product[:, :, 1, :].rearrange("p t (h d) -> p t h d", h=CHUNK_HEADS),
-                    op=ADD,
-                )
+            if which != V and result is not None:
+                if c in (1, 5) and b == B - 1:
+                    nc.vector.tensor_tensor(
+                        out=result[:].rearrange("p h t d -> p t h d"),
+                        in0=product[:, :, 0, :].rearrange("p t (h d) -> p t h d", h=CHUNK_HEADS),
+                        in1=product[:, :, 1, :].rearrange("p t (h d) -> p t h d", h=CHUNK_HEADS),
+                        op=ADD,
+                    )
+                else:
+                    for t in range(POS):
+                        nc.gpsimd.tensor_tensor(
+                            out=result[:, :, t, :],
+                            in0=product[:, t, 0, :].rearrange("p (h d) -> p h d", h=CHUNK_HEADS),
+                            in1=product[:, t, 1, :].rearrange("p (h d) -> p h d", h=CHUNK_HEADS),
+                            op=ADD,
+                        )
+            if result is not None:
+                store(c, b, result, nc.sync)
+
+        def store(c, b, result, queue):
+            which, half = chunks[c]
             first_head = half * CHUNK_HEADS
-            nc.sync.dma_start(
+            queue.dma_start(
                 out=outs[which][b, first_head : first_head + CHUNK_HEADS].rearrange(
                     "h (p t) d -> p h (t d)", t=POS
                 ),
                 in_=result[:].rearrange("p h t d -> p h (t d)"),
             )
+
+        def tensor_add(c, b):
+            product = held[(c, b)]
+            result = results.tile([P, CHUNK_HEADS, POS, HD], F32)
+            for t in range(POS):
+                total = v_banks.tile([P, CHUNK], F32, tag="v_bank")
+                for e in range(2):
+                    nc.tensor.matmul(
+                        out=total[:],
+                        lhsT=identity[:],
+                        rhs=product[:, t, e, :],
+                        start=(e == 0),
+                        stop=(e == 1),
+                    )
+                nc.scalar.copy(
+                    out=result[:, :, t, :],
+                    in_=total[:].rearrange("p (h d) -> p h d", h=CHUNK_HEADS),
+                )
+            store(c, b, result, nc.scalar)
 
         AHEAD = 2
         quantise_w(0)
@@ -204,3 +244,5 @@ def tile_ropeflashattention_pa_kernel(tc, x, w_qkv, cos, sin, out_0, out_1, out_
                 quantise_w(c + AHEAD)
             for b in range(B):
                 multiply(c, b)
+        for c, b in TENSOR_ADDS:
+            tensor_add(c, b)

@@ -55,23 +55,29 @@ def tile_ropeflashattention_pa_kernel(tc, x, w_qkv, cos, sin, out_0, out_1, out_
         def load_x(b):
             nc.sync.dma_start(out=x_sb[:, b], in_=x[b].rearrange("(p t) k -> p t k", t=POS))
 
-        def load_w(which, half):
-            col = which * D + half * CHUNK
+        w_chunk_rows = []
+        for which, half in chunks:
             rows = w_rows.tile([P, PASSES, PACK, CHUNK], BF16, name="rows")
-            for g in range(PASSES):
-                nc.sync.dma_start(
-                    out=rows[:, g],
-                    in_=w_qkv[g * K_PASS : (g + 1) * K_PASS, col : col + CHUNK].rearrange(
-                        "(p f) n -> p f n", f=PACK
-                    ),
-                )
-            return rows
+            w_chunk_rows.append(rows)
 
-        w_chunk_rows = [load_w(*chunks[0])]
-        for b in range(B):
+        def load_w(c, g):
+            which, half = chunks[c]
+            col = which * D + half * CHUNK
+            nc.sync.dma_start(
+                out=w_chunk_rows[c][:, g],
+                in_=w_qkv[g * K_PASS : (g + 1) * K_PASS, col : col + CHUNK].rearrange(
+                    "(p f) n -> p f n", f=PACK
+                ),
+            )
+
+        load_w(0, 0)
+        load_x(0)
+        load_w(0, 1)
+        for b in range(1, B):
             load_x(b)
-        for which, half in chunks[1:]:
-            w_chunk_rows.append(load_w(which, half))
+        for c in range(1, len(chunks)):
+            for g in range(PASSES):
+                load_w(c, g)
 
         identity = keep.tile([P, P], F32)
         make_identity(nc, identity[:])
@@ -79,8 +85,6 @@ def tile_ropeflashattention_pa_kernel(tc, x, w_qkv, cos, sin, out_0, out_1, out_
         rotation = keep.tile([P, POS, 2, PAIRS, 2], F32)
         nc.scalar.copy(out=rotation[:, :, 0, :, 0], in_=cos_sb[:])
         nc.scalar.copy(out=rotation[:, :, 0, :, 1], in_=sin_sb[:])
-        nc.vector.tensor_scalar_mul(out=rotation[:, :, 1, :, 0], in0=sin_sb[:], scalar1=-1.0)
-        nc.vector.tensor_copy(out=rotation[:, :, 1, :, 1], in_=cos_sb[:])
 
         x_grouped = keep.tile([P, TOKEN_TILES, PASSES, P, PACK], BF16, align_bytes=64)
         x_codes = keep.tile([P, TOKEN_TILES, PASSES, P], U32, align_bytes=64)
@@ -111,26 +115,37 @@ def tile_ropeflashattention_pa_kernel(tc, x, w_qkv, cos, sin, out_0, out_1, out_
                     in_=x_grouped[:, i].rearrange("p g m f -> p (g m f)"),
                 )
 
-        def quantise_w(c):
-            copy = nc.vector.tensor_copy if c == 0 else nc.scalar.copy
+        def regroup_w(c, g, copy):
+            copy(
+                out=w_groups[c][:, g].rearrange("p (n i) f -> p n f i", i=4),
+                in_=w_chunk_rows[c][:, g].rearrange("p f (n i) -> p n f i", i=4),
+            )
+
+        def quantise_w_pass(c, g):
+            nc.vector.quantize_mx(
+                out=w_codes[:, c, g, :].bitcast(FP8X4),
+                scales=w_scales[:, c, g, :],
+                in_=w_groups[c][:, g].rearrange("p n f -> p (n f)"),
+            )
+
+        w_groups = {}
+
+        def new_group(c):
             grouped = w_grouped.tile([P, PASSES, CHUNK, PACK], BF16, align_bytes=64)
+            w_groups[c] = grouped
+
+        def quantise_w(c):
+            new_group(c)
             for g in range(PASSES):
-                copy(
-                    out=grouped[:, g].rearrange("p (n i) f -> p n f i", i=4),
-                    in_=w_chunk_rows[c][:, g].rearrange("p f (n i) -> p n f i", i=4),
-                )
+                regroup_w(c, g, nc.scalar.copy)
             if c < 3:
                 for g in range(PASSES):
-                    nc.vector.quantize_mx(
-                        out=w_codes[:, c, g, :].bitcast(FP8X4),
-                        scales=w_scales[:, c, g, :],
-                        in_=grouped[:, g].rearrange("p n f -> p (n f)"),
-                    )
+                    quantise_w_pass(c, g)
             else:
                 nc.vector.quantize_mx(
                     out=w_codes[:, c].rearrange("p g n -> p (g n)").bitcast(FP8X4),
                     scales=w_scales[:, c].rearrange("p g n -> p (g n)"),
-                    in_=grouped[:].rearrange("p g n f -> p (g n f)"),
+                    in_=w_groups[c][:].rearrange("p g n f -> p (g n f)"),
                 )
 
         TENSOR_ADDS = ((3, B - 1),)
@@ -230,19 +245,45 @@ def tile_ropeflashattention_pa_kernel(tc, x, w_qkv, cos, sin, out_0, out_1, out_
             store(c, b, result, nc.scalar)
 
         AHEAD = 2
-        quantise_w(0)
-        for b in range(AHEAD):
-            quantise_x(b)
-        for b in range(B):
-            if b + AHEAD < B:
-                quantise_x(b + AHEAD)
-            else:
-                quantise_w(b + AHEAD - B + 1)
-            multiply(0, b)
-        for c in range(1, len(chunks)):
-            if c + AHEAD < len(chunks):
-                quantise_w(c + AHEAD)
+        with tc.manual_schedule(engines={mybir.EngineType.DVE}):
+            new_group(0)
+            regroup_w(0, 0, nc.vector.tensor_copy)
+            nc.vector.tensor_scalar_mul(out=rotation[:, :, 1, :, 0], in0=sin_sb[:], scalar1=-1.0)
+            nc.vector.tensor_copy(out=rotation[:, :, 1, :, 1], in_=cos_sb[:])
+            quantise_w_pass(0, 0)
+            regroup_w(0, 1, nc.vector.tensor_copy)
+        quantise_w_pass(0, 1)
+        with tc.manual_schedule(engines={mybir.EngineType.Activation}):
+            for b in range(AHEAD):
+                quantise_x(b)
             for b in range(B):
-                multiply(c, b)
+                if b + AHEAD < B:
+                    quantise_x(b + AHEAD)
+                else:
+                    quantise_w(b + AHEAD - B + 1)
+                multiply(0, b)
+        quantise_w(3)
+        multiply(1, 0)
+        multiply(1, 1)
+        multiply(2, 0)
+        multiply(1, 2)
+        quantise_w(4)
+        multiply(2, 1)
+        multiply(1, 3)
+        multiply(2, 2)
+        multiply(3, 0)
+        multiply(2, 3)
+        multiply(3, 1)
+        quantise_w(5)
+        multiply(3, 2)
+        multiply(4, 0)
+        multiply(3, 3)
+        multiply(4, 1)
+        multiply(5, 0)
+        multiply(4, 2)
+        multiply(5, 1)
+        multiply(4, 3)
+        multiply(5, 2)
+        multiply(5, 3)
         for c, b in TENSOR_ADDS:
             tensor_add(c, b)

from contextlib import ExitStack

import concourse.mybir as mybir
from concourse.masks import make_identity

F32 = mybir.dt.float32
BF16 = mybir.dt.bfloat16
U32 = mybir.dt.uint32
U8 = mybir.dt.uint8
FP8X4 = mybir.dt.float8_e4m3fn_x4
MULT = mybir.AluOpType.mult
ADD = mybir.AluOpType.add

B, S, H, HD = 4, 256, 8, 128
D = H * HD
PAIRS = HD // 2
P = 128
PACK = 4
K_PASS = P * PACK
PASSES = D // K_PASS
POS = S // P
TOKEN_TILES = B * POS
CHUNK = 512
CHUNK_HEADS = CHUNK // HD
HALVES = D // CHUNK
Q = 0
K = 1
V = 2

FLOPS = 2 * B * S * D * 3 * D


def tile_ropeflashattention_pa_kernel(tc, x, w_qkv, cos, sin, out_0, out_1, out_2):
    nc = tc.nc
    outs = (out_0, out_1, out_2)
    chunks = [(Q, 0), (K, 0), (V, 0), (Q, 1), (V, 1), (K, 1)]

    with ExitStack() as ctx:
        keep = ctx.enter_context(tc.tile_pool(name="keep", bufs=1))
        w_rows = ctx.enter_context(tc.tile_pool(name="w_rows", bufs=len(chunks)))
        w_grouped = ctx.enter_context(tc.tile_pool(name="w_grouped", bufs=2))
        products = ctx.enter_context(tc.tile_pool(name="products", bufs=4))
        results = ctx.enter_context(tc.tile_pool(name="results", bufs=6))
        v_results = ctx.enter_context(tc.tile_pool(name="v_results", bufs=B))
        banks = ctx.enter_context(tc.psum_pool(name="banks", bufs=6))
        v_banks = ctx.enter_context(tc.psum_pool(name="v_banks", bufs=2))

        cos_sb = keep.tile([P, POS, PAIRS], BF16)
        sin_sb = keep.tile([P, POS, PAIRS], BF16)
        nc.scalar.dma_start(out=cos_sb[:], in_=cos.rearrange("(p t) j -> p t j", t=POS))
        nc.scalar.dma_start(out=sin_sb[:], in_=sin.rearrange("(p t) j -> p t j", t=POS))

        x_sb = keep.tile([P, B, POS, D], BF16)

        def load_x(b):
            nc.sync.dma_start(out=x_sb[:, b], in_=x[b].rearrange("(p t) k -> p t k", t=POS))

        w_chunk_rows = []
        for which, half in chunks:
            rows = w_rows.tile([P, PASSES, PACK, CHUNK], BF16, name="rows")
            w_chunk_rows.append(rows)

        def load_w(c, g):
            which, half = chunks[c]
            col = which * D + half * CHUNK
            nc.sync.dma_start(
                out=w_chunk_rows[c][:, g],
                in_=w_qkv[g * K_PASS : (g + 1) * K_PASS, col : col + CHUNK].rearrange(
                    "(p f) n -> p f n", f=PACK
                ),
            )

        load_w(0, 0)
        load_x(0)
        load_w(0, 1)
        for b in range(1, B):
            load_x(b)
        for c in range(1, len(chunks)):
            for g in range(PASSES):
                load_w(c, g)

        identity = keep.tile([P, P], F32)
        make_identity(nc, identity[:])

        rotation = keep.tile([P, POS, 2, PAIRS, 2], F32)
        nc.scalar.copy(out=rotation[:, :, 0, :, 0], in_=cos_sb[:])
        nc.scalar.copy(out=rotation[:, :, 0, :, 1], in_=sin_sb[:])

        x_grouped = keep.tile([P, TOKEN_TILES, PASSES, P, PACK], BF16, align_bytes=64)
        x_codes = keep.tile([P, TOKEN_TILES, PASSES, P], U32, align_bytes=64)
        x_scales = keep.tile([P, TOKEN_TILES, PASSES, P], U8, align_bytes=64)
        w_codes = keep.tile([P, len(chunks), PASSES, CHUNK], U32, align_bytes=64)
        w_scales = keep.tile([P, len(chunks), PASSES, CHUNK], U8, align_bytes=64)

        def quantise_x(b):
            for t in range(POS):
                i = b * POS + t
                words = x_sb[:, b, t, :].bitcast(F32).rearrange(
                    "m (g p u) -> m g u p", g=PASSES, u=2
                )
                flipped = banks.tile([P, PASSES, 2, P], F32, tag="bank")
                for g in range(PASSES):
                    for u in range(2):
                        nc.tensor.transpose(flipped[:, g, u, :], words[:, g, u, :], identity[:])
                nc.scalar.copy(
                    out=x_grouped[:, i]
                    .rearrange("p g m f -> p (g m f)")
                    .bitcast(F32)
                    .rearrange("p (g m u) -> p g m u", g=PASSES, u=2),
                    in_=flipped[:].rearrange("p g u m -> p g m u"),
                )
                nc.vector.quantize_mx(
                    out=x_codes[:, i].rearrange("p g m -> p (g m)").bitcast(FP8X4),
                    scales=x_scales[:, i].rearrange("p g m -> p (g m)"),
                    in_=x_grouped[:, i].rearrange("p g m f -> p (g m f)"),
                )

        def regroup_w(c, g, copy):
            copy(
                out=w_groups[c][:, g].rearrange("p (n i) f -> p n f i", i=4),
                in_=w_chunk_rows[c][:, g].rearrange("p f (n i) -> p n f i", i=4),
            )

        def quantise_w_pass(c, g):
            nc.vector.quantize_mx(
                out=w_codes[:, c, g, :].bitcast(FP8X4),
                scales=w_scales[:, c, g, :],
                in_=w_groups[c][:, g].rearrange("p n f -> p (n f)"),
            )

        w_groups = {}

        def new_group(c):
            grouped = w_grouped.tile([P, PASSES, CHUNK, PACK], BF16, align_bytes=64)
            w_groups[c] = grouped

        def quantise_w(c):
            new_group(c)
            for g in range(PASSES):
                regroup_w(c, g, nc.scalar.copy)
            if c < 3:
                for g in range(PASSES):
                    quantise_w_pass(c, g)
            else:
                nc.vector.quantize_mx(
                    out=w_codes[:, c].rearrange("p g n -> p (g n)").bitcast(FP8X4),
                    scales=w_scales[:, c].rearrange("p g n -> p (g n)"),
                    in_=w_groups[c][:].rearrange("p g n f -> p (g n f)"),
                )

        TENSOR_ADDS = ((3, B - 1),)
        held = {}

        def multiply(c, b):
            which, half = chunks[c]
            product = None
            if which != V:
                product = products.tile([P, POS, 2, CHUNK], F32)
            if (c, b) in TENSOR_ADDS:
                result = None
                held[(c, b)] = product
            else:
                result_pool = v_results if which == V else results
                result = result_pool.tile([P, CHUNK_HEADS, POS, HD], F32)
            for t in range(POS):
                i = b * POS + t
                if which == V:
                    sums = v_banks.tile([P, CHUNK], F32, tag="v_bank")
                else:
                    sums = banks.tile([P, CHUNK], F32, tag="bank")
                for g in range(PASSES):
                    nc.tensor.matmul_mx(
                        out=sums[:],
                        lhsT=x_codes[:, i, g, :].bitcast(FP8X4),
                        lhsT_scale=x_scales[:, i, g, :],
                        rhs=w_codes[:, c, g, :].bitcast(FP8X4),
                        rhs_scale=w_scales[:, c, g, :],
                        start=(g == 0),
                        stop=(g == PASSES - 1),
                    )
                if which == V:
                    nc.scalar.copy(
                        out=result[:, :, t, :],
                        in_=sums[:].rearrange("p (h d) -> p h d", h=CHUNK_HEADS),
                    )
                else:
                    shape = [P, 2, CHUNK_HEADS, PAIRS, 2]
                    nc.vector.tensor_tensor(
                        out=product[:, t].rearrange(
                            "p e (h j r) -> p e h j r", h=CHUNK_HEADS, r=2
                        ),
                        in0=sums[:]
                        .rearrange("p (h j e) -> p e h j", h=CHUNK_HEADS, e=2)
                        .unsqueeze(4)
                        .to_broadcast(shape),
                        in1=rotation[:, t].unsqueeze(2).to_broadcast(shape),
                        op=MULT,
                    )
            if which != V and result is not None:
                if c in (1, 5) and b == B - 1:
                    nc.vector.tensor_tensor(
                        out=result[:].rearrange("p h t d -> p t h d"),
                        in0=product[:, :, 0, :].rearrange("p t (h d) -> p t h d", h=CHUNK_HEADS),
                        in1=product[:, :, 1, :].rearrange("p t (h d) -> p t h d", h=CHUNK_HEADS),
                        op=ADD,
                    )
                else:
                    for t in range(POS):
                        nc.gpsimd.tensor_tensor(
                            out=result[:, :, t, :],
                            in0=product[:, t, 0, :].rearrange("p (h d) -> p h d", h=CHUNK_HEADS),
                            in1=product[:, t, 1, :].rearrange("p (h d) -> p h d", h=CHUNK_HEADS),
                            op=ADD,
                        )
            if result is not None:
                store(c, b, result, nc.sync)

        def store(c, b, result, queue):
            which, half = chunks[c]
            first_head = half * CHUNK_HEADS
            queue.dma_start(
                out=outs[which][b, first_head : first_head + CHUNK_HEADS].rearrange(
                    "h (p t) d -> p h (t d)", t=POS
                ),
                in_=result[:].rearrange("p h t d -> p h (t d)"),
            )

        def tensor_add(c, b):
            product = held[(c, b)]
            result = results.tile([P, CHUNK_HEADS, POS, HD], F32)
            for t in range(POS):
                total = v_banks.tile([P, CHUNK], F32, tag="v_bank")
                for e in range(2):
                    nc.tensor.matmul(
                        out=total[:],
                        lhsT=identity[:],
                        rhs=product[:, t, e, :],
                        start=(e == 0),
                        stop=(e == 1),
                    )
                nc.scalar.copy(
                    out=result[:, :, t, :],
                    in_=total[:].rearrange("p (h d) -> p h d", h=CHUNK_HEADS),
                )
            store(c, b, result, nc.scalar)

        AHEAD = 2
        with tc.manual_schedule(engines={mybir.EngineType.DVE}):
            new_group(0)
            regroup_w(0, 0, nc.vector.tensor_copy)
            nc.vector.tensor_scalar_mul(out=rotation[:, :, 1, :, 0], in0=sin_sb[:], scalar1=-1.0)
            nc.vector.tensor_copy(out=rotation[:, :, 1, :, 1], in_=cos_sb[:])
            quantise_w_pass(0, 0)
            regroup_w(0, 1, nc.vector.tensor_copy)
        quantise_w_pass(0, 1)
        with tc.manual_schedule(engines={mybir.EngineType.Activation}):
            for b in range(AHEAD):
                quantise_x(b)
            for b in range(B):
                if b + AHEAD < B:
                    quantise_x(b + AHEAD)
                else:
                    quantise_w(b + AHEAD - B + 1)
                multiply(0, b)
        quantise_w(3)
        multiply(1, 0)
        multiply(1, 1)
        multiply(2, 0)
        multiply(1, 2)
        quantise_w(4)
        multiply(2, 1)
        multiply(1, 3)
        multiply(2, 2)
        multiply(3, 0)
        multiply(2, 3)
        multiply(3, 1)
        quantise_w(5)
        multiply(3, 2)
        multiply(4, 0)
        multiply(3, 3)
        multiply(4, 1)
        multiply(5, 0)
        multiply(4, 2)
        multiply(5, 1)
        multiply(4, 3)
        multiply(5, 2)
        multiply(5, 3)
        for c, b in TENSOR_ADDS:
            tensor_add(c, b)
